import numpy as np
import ml_dtypes


def mxq(x, axis, fmt="e4m3"):
    dtype, down = {"e4m3": (ml_dtypes.float8_e4m3fn, 7), "e5m2": (ml_dtypes.float8_e5m2, 14)}[fmt]
    v = np.moveaxis(np.asarray(x, np.float32).astype(ml_dtypes.bfloat16).astype(np.float64), axis, -1)
    blocks = v.reshape(v.shape[:-1] + (-1, 32))
    amax = np.abs(blocks).max(-1, keepdims=True)
    byte = np.maximum(np.where(amax > 0, np.frexp(amax)[1] - 1 + 127, 0) - down, 1)
    scale = np.exp2(byte - 127.0)
    codes = (blocks / scale).astype(np.float32).astype(dtype).astype(np.float64)
    return np.moveaxis((codes * scale).reshape(v.shape), -1, axis)


WIDE = False


def mx_kscale(k):
    if not WIDE:
        return np.ones(k)
    levels = np.array([10, -10, 5, -5, 0])
    a = np.random.permutation(np.resize(levels, k // 512 * 4)).reshape(k // 512, 4)
    idx = np.arange(k)
    return np.exp2(a[idx // 512, idx % 128 // 32])


BF16 = ml_dtypes.bfloat16


def bf(x):
    return np.asarray(x, np.float32).astype(BF16)


def f64(x):
    return np.asarray(x).astype(np.float64)


E2M1 = np.array([0.0, 0.5, 1.0, 1.5, 2.0, 3.0, 4.0, 6.0, -0.0, -0.5, -1.0, -1.5, -2.0, -3.0, -4.0, -6.0])


def pack_weight(w, fmt):
    k, n = w.shape
    w = f64(bf(w)).reshape(k // 32, 32, n)
    amax = np.abs(w).max(1)
    if fmt == "e4m3":
        byte = np.frexp(amax)[1] - 1 + 127 - 7
    else:
        mant, ex = np.frexp(amax / 6.0)
        byte = np.where(mant > 0.5, ex, ex - 1) + 127
    byte = np.clip(np.where(amax > 0, byte, 1), 1, 254)
    scaled = (w * np.exp2(127.0 - byte)[:, None, :]).reshape(k, n).astype(np.float32)
    by_word = np.ascontiguousarray(scaled.reshape(k // 512, 128, 4, n).transpose(0, 1, 3, 2))
    if fmt == "e4m3":
        words = by_word.astype(ml_dtypes.float8_e4m3fn).view(np.uint8)
    else:
        c = by_word.astype(ml_dtypes.float4_e2m1fn).view(np.uint8) & 0xF
        words = c[..., 0::2] | (c[..., 1::2] << 4)
    return np.ascontiguousarray(words), np.ascontiguousarray(byte.astype(np.uint8).reshape(k // 512, 16, n))


def unpack_weight(words, scales, fmt):
    g, p, n, _ = words.shape
    if fmt == "e4m3":
        vals = np.ascontiguousarray(words).view(ml_dtypes.float8_e4m3fn).astype(np.float64)
    else:
        nib = np.empty((g, p, n, 4), np.uint8)
        nib[..., 0::2] = words & 0xF
        nib[..., 1::2] = words >> 4
        vals = E2M1[nib]
    vals = vals * np.repeat(np.exp2(scales.astype(np.float64) - 127.0), 8, axis=1)[..., None]
    return vals.transpose(0, 1, 3, 2).reshape(g * 512, n)


S, N, C, O = 9, 2048, 512, 512
K = S * C


def setup_inputs():
    s = mx_kscale(K).reshape(S, C)
    inp = {f"x{i}": bf(np.random.standard_normal((N, C)) * s[i]) for i in range(S)}
    stack = (np.random.standard_normal((S, O, C)) / np.sqrt(K) / s[:, None, :]).swapaxes(1, 2)
    cat = stack.reshape(-1, O)
    words, scales = pack_weight(cat, "e4m3")
    inp["weights_words"] = words
    inp["weights_scales"] = scales
    inp["bias"] = bf(np.random.standard_normal((S, O)) * 0.3)
    return inp


def reference(x0, x1, x2, x3, x4, x5, x6, x7, x8, weights_words, weights_scales, bias):
    xs = np.stack([f64(x0), f64(x1), f64(x2), f64(x3), f64(x4), f64(x5), f64(x6), f64(x7), f64(x8)], axis=0)
    xc = xs.transpose(1, 0, 2).reshape(N, K)
    wc = unpack_weight(weights_words, weights_scales, "e4m3").reshape(S, C, O).reshape(K, O)
    out = mxq(xc, 1, "e4m3") @ wc
    out = out + np.sum(f64(bias), axis=0)
    return out

@@ -1,0 +1,204 @@
+from contextlib import ExitStack
+
+import concourse.mybir as mybir
+from concourse.masks import make_identity
+
+F32 = mybir.dt.float32
+BF16 = mybir.dt.bfloat16
+I32 = mybir.dt.int32
+U32 = mybir.dt.uint32
+U8 = mybir.dt.uint8
+FP8X4 = mybir.dt.float8_e4m3fn_x4
+
+P = 128
+PACK = 4
+HALVES = 2
+SLOTS = 9
+ROWS = 2048
+C_IN = 512
+C_OUT = 512
+ROW_TILES = ROWS // P
+SCALE_ROWS = 16
+QUADRANTS = 4
+
+TILES_PER_CHUNK = 4
+CHUNKS = ROW_TILES // TILES_PER_CHUNK
+TILES_PER_BANK = 2
+
+SLOTS_PER_ROUND = 2
+LOAD_AHEAD = 6
+
+FLOPS = 2 * ROWS * SLOTS * C_IN * C_OUT
+
+
+def tile_scattervertical_e_kernel(
+    tc, x0, x1, x2, x3, x4, x5, x6, x7, x8, weights_words, weights_scales, bias, out
+):
+    nc = tc.nc
+    x_rows = [
+        x.rearrange("(p t) c -> p t c", t=ROW_TILES) for x in (x0, x1, x2, x3, x4, x5, x6, x7, x8)
+    ]
+    out_rows = out.rearrange("(p t) o -> p t o", t=ROW_TILES)
+
+    rounds = []
+    for chunk in range(CHUNKS):
+        for first_slot in range(0, SLOTS, SLOTS_PER_ROUND):
+            last_slot = min(first_slot + SLOTS_PER_ROUND, SLOTS)
+            rounds.append([(chunk, slot) for slot in range(first_slot, last_slot)])
+    n_rounds = len(rounds)
+
+    with ExitStack() as ctx:
+        ctx.enter_context(tc.manual_schedule())
+        keep = ctx.enter_context(tc.tile_pool(name="keep", bufs=1))
+        raw_pool = ctx.enter_context(tc.tile_pool(name="raw", bufs=LOAD_AHEAD * SLOTS_PER_ROUND))
+        sorted_pool = ctx.enter_context(tc.tile_pool(name="sorted", bufs=3 * SLOTS_PER_ROUND))
+        grouped_pool = ctx.enter_context(tc.tile_pool(name="grouped", bufs=2 * SLOTS_PER_ROUND))
+        codes_pool = ctx.enter_context(tc.tile_pool(name="codes", bufs=3 * SLOTS_PER_ROUND))
+        result_pool = ctx.enter_context(tc.tile_pool(name="result", bufs=2 * TILES_PER_CHUNK))
+        turned_pool = ctx.enter_context(tc.psum_pool(name="turned", bufs=4))
+        sums_pool = ctx.enter_context(tc.psum_pool(name="sums", bufs=TILES_PER_CHUNK))
+
+        identity = keep.tile([P, P], F32)
+        make_identity(nc, identity[:])
+
+        w_codes = keep.tile([P, SLOTS, C_OUT * PACK], U8, align_bytes=64)
+        w_scales = keep.tile([P, SLOTS, C_OUT], U8, align_bytes=64)
+        nc.vector.memset(w_scales[:].bitcast(I32), 0)
+
+        bias_rows = keep.tile([P, C_OUT], BF16)
+        ones = keep.tile([P, P], BF16)
+        bias_sum = keep.tile([P, C_OUT], F32)
+        nc.vector.memset(bias_rows[:].bitcast(I32), 0)
+        nc.vector.memset(ones[:], 1.0)
+        nc.scalar.dma_start(out=bias_rows[0:SLOTS, :], in_=bias)
+        bias_bank = sums_pool.tile([P, C_OUT], F32, name="sums")
+        nc.tensor.matmul(out=bias_bank[:], lhsT=ones[:], rhs=bias_rows[:], start=True, stop=True)
+        nc.scalar.copy(out=bias_sum[:], in_=bias_bank[:])
+
+        raw_tiles = {}
+        sorted_tiles = {}
+        grouped_tiles = {}
+        code_tiles = {}
+        sums = {}
+
+        def load_x(step):
+            chunk, slot = step
+            first = chunk * TILES_PER_CHUNK
+            raw = raw_pool.tile([P, TILES_PER_CHUNK, C_IN], BF16)
+            nc.sync.dma_start(out=raw[:], in_=x_rows[slot][:, first : first + TILES_PER_CHUNK, :])
+            raw_tiles[step] = raw
+
+        def load_scale_rows():
+            for quadrant in range(QUADRANTS):
+                nc.sync.dma_start(
+                    out=w_scales[32 * quadrant : 32 * quadrant + 4, :, :].bitcast(I32),
+                    in_=weights_scales[:, 4 * quadrant : 4 * quadrant + 4, :]
+                    .rearrange("g r n -> r g n")
+                    .bitcast(I32),
+                )
+
+        def load_codes(slot):
+            nc.sync.dma_start(
+                out=w_codes[:, slot, :].bitcast(I32),
+                in_=weights_words[slot].rearrange("p n t -> p (n t)").bitcast(I32),
+            )
+
+        def load_round(r):
+            for step in rounds[r]:
+                load_x(step)
+            if r == 1:
+                load_scale_rows()
+            if r >= 1:
+                for chunk, slot in rounds[r - 1]:
+                    if chunk == 0:
+                        load_codes(slot)
+
+        def sort_words(step):
+            words = raw_tiles[step][:].rearrange("p i c -> p (i c)").bitcast(F32)
+            sorted_words = sorted_pool.tile([P, TILES_PER_CHUNK, HALVES, P], F32)
+            nc.vector.tensor_copy(
+                out=sorted_words[:],
+                in_=words.rearrange("p (i j u) -> p i u j", i=TILES_PER_CHUNK, u=HALVES),
+            )
+            sorted_tiles[step] = sorted_words
+
+        def turn(step):
+            grouped = grouped_pool.tile([P, TILES_PER_CHUNK, P, PACK], BF16, align_bytes=64)
+            grouped_words = (
+                grouped[:]
+                .rearrange("p i r t -> p (i r t)")
+                .bitcast(F32)
+                .rearrange("p (i r u) -> p i r u", i=TILES_PER_CHUNK, u=HALVES)
+            )
+            for first in range(0, TILES_PER_CHUNK, TILES_PER_BANK):
+                turned = turned_pool.tile([P, TILES_PER_BANK, HALVES, P], F32)
+                for i in range(TILES_PER_BANK):
+                    for u in range(HALVES):
+                        nc.tensor.transpose(
+                            turned[:, i, u, :], sorted_tiles[step][:, first + i, u, :], identity[:]
+                        )
+                nc.scalar.copy(
+                    out=grouped_words[:, first : first + TILES_PER_BANK, :, :],
+                    in_=turned[:].rearrange("p i u r -> p i r u"),
+                )
+            grouped_tiles[step] = grouped
+
+        def quantise(step):
+            x_codes = codes_pool.tile([P, TILES_PER_CHUNK * P], U32, align_bytes=64)
+            x_scales = codes_pool.tile([P, TILES_PER_CHUNK * P], U8, align_bytes=64)
+            nc.vector.quantize_mx(
+                out=x_codes[:].bitcast(FP8X4),
+                scales=x_scales[:],
+                in_=grouped_tiles[step][:].rearrange("p i r t -> p (i r t)"),
+            )
+            code_tiles[step] = (x_codes, x_scales)
+
+        def multiply(step):
+            chunk, slot = step
+            x_codes, x_scales = code_tiles[step]
+            for i in range(TILES_PER_CHUNK):
+                if slot == 0:
+                    sums[(chunk, i)] = sums_pool.tile([P, C_OUT], F32, name="sums")
+                rows = slice(i * P, (i + 1) * P)
+                nc.tensor.matmul_mx(
+                    out=sums[(chunk, i)][:],
+                    lhsT=x_codes[:, rows].bitcast(FP8X4),
+                    lhsT_scale=x_scales[:, rows],
+                    rhs=w_codes[:, slot, :].bitcast(FP8X4),
+                    rhs_scale=w_scales[:, slot, :],
+                    start=(slot == 0),
+                    stop=(slot == SLOTS - 1),
+                )
+
+        def finish(chunk):
+            for i in range(TILES_PER_CHUNK):
+                result = result_pool.tile([P, C_OUT], F32)
+                nc.vector.tensor_tensor(
+                    out=result[:], in0=sums[(chunk, i)][:], in1=bias_sum[:], op=mybir.AluOpType.add
+                )
+                nc.sync.dma_start(out=out_rows[:, chunk * TILES_PER_CHUNK + i, :], in_=result[:])
+
+        for r in range(LOAD_AHEAD):
+            load_round(r)
+        for step in rounds[0]:
+            sort_words(step)
+        for r in range(n_rounds + 2):
+            if r + LOAD_AHEAD < n_rounds:
+                load_round(r + LOAD_AHEAD)
+            if r >= 2:
+                chunk, slot = rounds[r - 2][-1]
+                if slot == SLOTS - 1:
+                    finish(chunk)
+            if r < n_rounds:
+                for step in rounds[r]:
+                    turn(step)
+            if 1 <= r <= n_rounds:
+                for step in rounds[r - 1]:
+                    multiply(step)
+            to_sort = rounds[r + 1] if r + 1 < n_rounds else []
+            to_quantise = rounds[r] if r < n_rounds else []
+            for k in range(SLOTS_PER_ROUND):
+                if k < len(to_sort):
+                    sort_words(to_sort[k])
+                if k < len(to_quantise):
+                    quantise(to_quantise[k])

@@ -27,6 +27,7 @@ TILES_PER_BANK = 2
 
 SLOTS_PER_ROUND = 2
 LOAD_AHEAD = 6
+BIAS_TURN = 2
 
 FLOPS = 2 * ROWS * SLOTS * C_IN * C_OUT
 
@@ -40,11 +41,11 @@ def tile_scattervertical_e_kernel(
     ]
     out_rows = out.rearrange("(p t) o -> p t o", t=ROW_TILES)
 
+    cuts = sorted(set([0] + list(range(SLOTS % SLOTS_PER_ROUND, SLOTS + 1, SLOTS_PER_ROUND))))
     rounds = []
     for chunk in range(CHUNKS):
-        for first_slot in range(0, SLOTS, SLOTS_PER_ROUND):
-            last_slot = min(first_slot + SLOTS_PER_ROUND, SLOTS)
-            rounds.append([(chunk, slot) for slot in range(first_slot, last_slot)])
+        for first_slot, end_slot in zip(cuts, cuts[1:]):
+            rounds.append([(chunk, slot) for slot in range(first_slot, end_slot)])
     n_rounds = len(rounds)
 
     with ExitStack() as ctx:
@@ -71,9 +72,13 @@ def tile_scattervertical_e_kernel(
         nc.vector.memset(bias_rows[:].bitcast(I32), 0)
         nc.vector.memset(ones[:], 1.0)
         nc.scalar.dma_start(out=bias_rows[0:SLOTS, :], in_=bias)
-        bias_bank = sums_pool.tile([P, C_OUT], F32, name="sums")
-        nc.tensor.matmul(out=bias_bank[:], lhsT=ones[:], rhs=bias_rows[:], start=True, stop=True)
-        nc.scalar.copy(out=bias_sum[:], in_=bias_bank[:])
+
+        def sum_biases():
+            bias_bank = turned_pool.tile([P, C_OUT], F32, name="turned")
+            nc.tensor.matmul(
+                out=bias_bank[:], lhsT=ones[:], rhs=bias_rows[:], start=True, stop=True
+            )
+            nc.scalar.copy(out=bias_sum[:], in_=bias_bank[:])
 
         raw_tiles = {}
         sorted_tiles = {}
@@ -153,22 +158,22 @@ def tile_scattervertical_e_kernel(
             )
             code_tiles[step] = (x_codes, x_scales)
 
-        def multiply(step):
-            chunk, slot = step
-            x_codes, x_scales = code_tiles[step]
+        def multiply(steps):
             for i in range(TILES_PER_CHUNK):
-                if slot == 0:
-                    sums[(chunk, i)] = sums_pool.tile([P, C_OUT], F32, name="sums")
                 rows = slice(i * P, (i + 1) * P)
-                nc.tensor.matmul_mx(
-                    out=sums[(chunk, i)][:],
-                    lhsT=x_codes[:, rows].bitcast(FP8X4),
-                    lhsT_scale=x_scales[:, rows],
-                    rhs=w_codes[:, slot, :].bitcast(FP8X4),
-                    rhs_scale=w_scales[:, slot, :],
-                    start=(slot == 0),
-                    stop=(slot == SLOTS - 1),
-                )
+                for chunk, slot in steps:
+                    if slot == 0:
+                        sums[(chunk, i)] = sums_pool.tile([P, C_OUT], F32, name="sums")
+                    x_codes, x_scales = code_tiles[(chunk, slot)]
+                    nc.tensor.matmul_mx(
+                        out=sums[(chunk, i)][:],
+                        lhsT=x_codes[:, rows].bitcast(FP8X4),
+                        lhsT_scale=x_scales[:, rows],
+                        rhs=w_codes[:, slot, :].bitcast(FP8X4),
+                        rhs_scale=w_scales[:, slot, :],
+                        start=(slot == 0),
+                        stop=(slot == SLOTS - 1),
+                    )
 
         def finish(chunk):
             for i in range(TILES_PER_CHUNK):
@@ -193,8 +198,9 @@ def tile_scattervertical_e_kernel(
                 for step in rounds[r]:
                     turn(step)
             if 1 <= r <= n_rounds:
-                for step in rounds[r - 1]:
-                    multiply(step)
+                multiply(rounds[r - 1])
+            if r == BIAS_TURN:
+                sum_biases()
             to_sort = rounds[r + 1] if r + 1 < n_rounds else []
             to_quantise = rounds[r] if r < n_rounds else []
             for k in range(SLOTS_PER_ROUND):

@@ -70,8 +70,9 @@ def tile_scattervertical_e_kernel(
         ones = keep.tile([P, P], BF16)
         bias_sum = keep.tile([P, C_OUT], F32)
         nc.vector.memset(bias_rows[:].bitcast(I32), 0)
-        nc.vector.memset(ones[:], 1.0)
-        nc.scalar.dma_start(out=bias_rows[0:SLOTS, :], in_=bias)
+        nc.gpsimd.memset(ones[:], 1.0)
+        first_copy = keep.tile([P, 1], BF16)
+        nc.scalar.copy(out=first_copy[:], in_=ones[:, 0:1])
 
         def sum_biases():
             bias_bank = turned_pool.tile([P, C_OUT], F32, name="turned")
@@ -113,6 +114,8 @@ def tile_scattervertical_e_kernel(
                 load_x(step)
             if r == 1:
                 load_scale_rows()
+            if r == 2:
+                nc.sync.dma_start(out=bias_rows[0:SLOTS, :], in_=bias)
             if r >= 1:
                 for chunk, slot in rounds[r - 1]:
                     if chunk == 0:
@@ -203,8 +206,7 @@ def tile_scattervertical_e_kernel(
                 sum_biases()
             to_sort = rounds[r + 1] if r + 1 < n_rounds else []
             to_quantise = rounds[r] if r < n_rounds else []
-            for k in range(SLOTS_PER_ROUND):
-                if k < len(to_sort):
-                    sort_words(to_sort[k])
-                if k < len(to_quantise):
-                    quantise(to_quantise[k])
+            for step in to_sort:
+                sort_words(step)
+            for step in to_quantise:
+                quantise(step)

@@ -21,11 +21,16 @@ ROW_TILES = ROWS // P
 SCALE_ROWS = 16
 QUADRANTS = 4
 
-TILES_PER_CHUNK = 4
-CHUNKS = ROW_TILES // TILES_PER_CHUNK
-TILES_PER_BANK = 2
+CHUNK_TILES = [4, 2, 2, 2, 2, 2, 2]
+CHUNK_FIRST = [sum(CHUNK_TILES[:c]) for c in range(len(CHUNK_TILES))]
+UNITS_PER_BANK = 2
+UNITS_PER_COPY = 4
 
-SLOTS_PER_ROUND = 2
+WIDE_CUTS = [0, 1, 3, 5, 7, 9]
+NARROW_CUTS = [0, 4, 9]
+MAX_UNITS = 10
+WIDE_BANKS = [4, 5, 6, 7]
+NARROW_BANKS = [4, 5, 6, 7, 0, 1]
 LOAD_AHEAD = 6
 BIAS_TURN = 2
 
@@ -41,23 +46,21 @@ def tile_scattervertical_e_kernel(
     ]
     out_rows = out.rearrange("(p t) o -> p t o", t=ROW_TILES)
 
-    cuts = sorted(set([0] + list(range(SLOTS % SLOTS_PER_ROUND, SLOTS + 1, SLOTS_PER_ROUND))))
     rounds = []
-    for chunk in range(CHUNKS):
-        for first_slot, end_slot in zip(cuts, cuts[1:]):
-            rounds.append([(chunk, slot) for slot in range(first_slot, end_slot)])
+    for chunk, n_tiles in enumerate(CHUNK_TILES):
+        cuts = WIDE_CUTS if n_tiles == 4 else NARROW_CUTS
+        rounds.extend([(chunk, a, b) for a, b in zip(cuts, cuts[1:])])
     n_rounds = len(rounds)
 
     with ExitStack() as ctx:
         ctx.enter_context(tc.manual_schedule())
         keep = ctx.enter_context(tc.tile_pool(name="keep", bufs=1))
-        raw_pool = ctx.enter_context(tc.tile_pool(name="raw", bufs=LOAD_AHEAD * SLOTS_PER_ROUND))
-        sorted_pool = ctx.enter_context(tc.tile_pool(name="sorted", bufs=3 * SLOTS_PER_ROUND))
-        grouped_pool = ctx.enter_context(tc.tile_pool(name="grouped", bufs=2 * SLOTS_PER_ROUND))
-        codes_pool = ctx.enter_context(tc.tile_pool(name="codes", bufs=3 * SLOTS_PER_ROUND))
-        result_pool = ctx.enter_context(tc.tile_pool(name="result", bufs=2 * TILES_PER_CHUNK))
-        turned_pool = ctx.enter_context(tc.psum_pool(name="turned", bufs=4))
-        sums_pool = ctx.enter_context(tc.psum_pool(name="sums", bufs=TILES_PER_CHUNK))
+        raw_pool = ctx.enter_context(tc.tile_pool(name="raw", bufs=4))
+        sorted_pool = ctx.enter_context(tc.tile_pool(name="sorted", bufs=2))
+        grouped_pool = ctx.enter_context(tc.tile_pool(name="grouped", bufs=2))
+        codes_pool = ctx.enter_context(tc.tile_pool(name="codes", bufs=2))
+        result_pool = ctx.enter_context(tc.tile_pool(name="result", bufs=4))
+        psum = ctx.enter_context(tc.psum_pool(name="psum", bufs=1))
 
         identity = keep.tile([P, P], F32)
         make_identity(nc, identity[:])
@@ -74,8 +77,22 @@ def tile_scattervertical_e_kernel(
         first_copy = keep.tile([P, 1], BF16)
         nc.scalar.copy(out=first_copy[:], in_=ones[:, 0:1])
 
+        turns_made = {"wide": 0, "narrow": 0}
+
+        def open_bank(number):
+            return psum.tile([P, C_OUT], F32, name="bank%d" % number)
+
+        def next_turn_bank(chunk):
+            kind, banks = ("wide", WIDE_BANKS) if chunk == 0 else ("narrow", NARROW_BANKS)
+            number = banks[turns_made[kind] % len(banks)]
+            turns_made[kind] += 1
+            return open_bank(number)
+
+        def sum_bank(chunk, i):
+            return open_bank(i if chunk == 0 else 2 + i)
+
         def sum_biases():
-            bias_bank = turned_pool.tile([P, C_OUT], F32, name="turned")
+            bias_bank = next_turn_bank(0)
             nc.tensor.matmul(
                 out=bias_bank[:], lhsT=ones[:], rhs=bias_rows[:], start=True, stop=True
             )
@@ -87,12 +104,17 @@ def tile_scattervertical_e_kernel(
         code_tiles = {}
         sums = {}
 
-        def load_x(step):
-            chunk, slot = step
-            first = chunk * TILES_PER_CHUNK
-            raw = raw_pool.tile([P, TILES_PER_CHUNK, C_IN], BF16)
-            nc.sync.dma_start(out=raw[:], in_=x_rows[slot][:, first : first + TILES_PER_CHUNK, :])
-            raw_tiles[step] = raw
+        def load_x(chunk, slot):
+            first, n_tiles = CHUNK_FIRST[chunk], CHUNK_TILES[chunk]
+            if slot == 0:
+                if chunk == 0:
+                    raw_tiles[chunk] = keep.tile([P, SLOTS, n_tiles, C_IN], BF16, name="wide_raw")
+                else:
+                    raw_tiles[chunk] = raw_pool.tile([P, SLOTS, n_tiles, C_IN], BF16, name="raw")
+            nc.sync.dma_start(
+                out=raw_tiles[chunk][:, slot, :, :],
+                in_=x_rows[slot][:, first : first + n_tiles, :],
+            )
 
         def load_scale_rows():
             for quadrant in range(QUADRANTS):
@@ -110,68 +132,84 @@ def tile_scattervertical_e_kernel(
             )
 
         def load_round(r):
-            for step in rounds[r]:
-                load_x(step)
+            chunk, a, b = rounds[r]
+            for slot in range(a, b):
+                load_x(chunk, slot)
             if r == 1:
                 load_scale_rows()
             if r == 2:
                 nc.sync.dma_start(out=bias_rows[0:SLOTS, :], in_=bias)
             if r >= 1:
-                for chunk, slot in rounds[r - 1]:
-                    if chunk == 0:
+                chunk, a, b = rounds[r - 1]
+                if chunk == 0:
+                    for slot in range(a, b):
                         load_codes(slot)
 
-        def sort_words(step):
-            words = raw_tiles[step][:].rearrange("p i c -> p (i c)").bitcast(F32)
-            sorted_words = sorted_pool.tile([P, TILES_PER_CHUNK, HALVES, P], F32)
-            nc.vector.tensor_copy(
-                out=sorted_words[:],
-                in_=words.rearrange("p (i j u) -> p i u j", i=TILES_PER_CHUNK, u=HALVES),
-            )
-            sorted_tiles[step] = sorted_words
+        def sort_round(r):
+            chunk, a, b = rounds[r]
+            n_tiles = CHUNK_TILES[chunk]
+            sorted_words = sorted_pool.tile([P, MAX_UNITS, HALVES, P], F32)
+            slots = UNITS_PER_COPY // n_tiles
+            for s in range(a, b, slots):
+                e = min(s + slots, b)
+                words = raw_tiles[chunk][:, s:e, :, :].rearrange("p s i c -> p (s i c)").bitcast(F32)
+                nc.vector.tensor_copy(
+                    out=sorted_words[:, (s - a) * n_tiles : (e - a) * n_tiles, :, :],
+                    in_=words.rearrange("p (k j u) -> p k u j", j=P, u=HALVES),
+                )
+            sorted_tiles[r] = sorted_words
 
-        def turn(step):
-            grouped = grouped_pool.tile([P, TILES_PER_CHUNK, P, PACK], BF16, align_bytes=64)
+        def n_units(r):
+            chunk, a, b = rounds[r]
+            return (b - a) * CHUNK_TILES[chunk]
+
+        def turn_round(r):
+            grouped = grouped_pool.tile([P, MAX_UNITS, P, PACK], BF16, align_bytes=64)
             grouped_words = (
                 grouped[:]
-                .rearrange("p i r t -> p (i r t)")
+                .rearrange("p k r t -> p (k r t)")
                 .bitcast(F32)
-                .rearrange("p (i r u) -> p i r u", i=TILES_PER_CHUNK, u=HALVES)
+                .rearrange("p (k r u) -> p k r u", k=MAX_UNITS, u=HALVES)
             )
-            for first in range(0, TILES_PER_CHUNK, TILES_PER_BANK):
-                turned = turned_pool.tile([P, TILES_PER_BANK, HALVES, P], F32)
-                for i in range(TILES_PER_BANK):
+            for first in range(0, n_units(r), UNITS_PER_BANK):
+                bank = next_turn_bank(rounds[r][0])
+                turned = bank[:].rearrange("p (k u r) -> p k u r", k=UNITS_PER_BANK, u=HALVES)
+                for k in range(UNITS_PER_BANK):
                     for u in range(HALVES):
                         nc.tensor.transpose(
-                            turned[:, i, u, :], sorted_tiles[step][:, first + i, u, :], identity[:]
+                            turned[:, k, u, :], sorted_tiles[r][:, first + k, u, :], identity[:]
                         )
                 nc.scalar.copy(
-                    out=grouped_words[:, first : first + TILES_PER_BANK, :, :],
-                    in_=turned[:].rearrange("p i u r -> p i r u"),
+                    out=grouped_words[:, first : first + UNITS_PER_BANK, :, :],
+                    in_=turned.rearrange("p k u r -> p k r u"),
                 )
-            grouped_tiles[step] = grouped
+            grouped_tiles[r] = grouped
 
-        def quantise(step):
-            x_codes = codes_pool.tile([P, TILES_PER_CHUNK * P], U32, align_bytes=64)
-            x_scales = codes_pool.tile([P, TILES_PER_CHUNK * P], U8, align_bytes=64)
-            nc.vector.quantize_mx(
-                out=x_codes[:].bitcast(FP8X4),
-                scales=x_scales[:],
-                in_=grouped_tiles[step][:].rearrange("p i r t -> p (i r t)"),
-            )
-            code_tiles[step] = (x_codes, x_scales)
+        def quantise_round(r):
+            x_codes = codes_pool.tile([P, MAX_UNITS, P], U32, align_bytes=64)
+            x_scales = codes_pool.tile([P, MAX_UNITS, P], U8, align_bytes=64)
+            for first in range(0, n_units(r), UNITS_PER_COPY):
+                units = slice(first, min(first + UNITS_PER_COPY, n_units(r)))
+                nc.vector.quantize_mx(
+                    out=x_codes[:, units, :].rearrange("p k r -> p (k r)").bitcast(FP8X4),
+                    scales=x_scales[:, units, :].rearrange("p k r -> p (k r)"),
+                    in_=grouped_tiles[r][:, units, :, :].rearrange("p k r t -> p (k r t)"),
+                )
+            code_tiles[r] = (x_codes, x_scales)
 
-        def multiply(steps):
-            for i in range(TILES_PER_CHUNK):
-                rows = slice(i * P, (i + 1) * P)
-                for chunk, slot in steps:
+        def multiply_round(r):
+            chunk, a, b = rounds[r]
+            n_tiles = CHUNK_TILES[chunk]
+            x_codes, x_scales = code_tiles[r]
+            for i in range(n_tiles):
+                for slot in range(a, b):
                     if slot == 0:
-                        sums[(chunk, i)] = sums_pool.tile([P, C_OUT], F32, name="sums")
-                    x_codes, x_scales = code_tiles[(chunk, slot)]
+                        sums[(chunk, i)] = sum_bank(chunk, i)
+                    k = (slot - a) * n_tiles + i
                     nc.tensor.matmul_mx(
                         out=sums[(chunk, i)][:],
-                        lhsT=x_codes[:, rows].bitcast(FP8X4),
-                        lhsT_scale=x_scales[:, rows],
+                        lhsT=x_codes[:, k, :].bitcast(FP8X4),
+                        lhsT_scale=x_scales[:, k, :],
                         rhs=w_codes[:, slot, :].bitcast(FP8X4),
                         rhs_scale=w_scales[:, slot, :],
                         start=(slot == 0),
@@ -179,34 +217,28 @@ def tile_scattervertical_e_kernel(
                     )
 
         def finish(chunk):
-            for i in range(TILES_PER_CHUNK):
+            for i in range(CHUNK_TILES[chunk]):
                 result = result_pool.tile([P, C_OUT], F32)
                 nc.vector.tensor_tensor(
                     out=result[:], in0=sums[(chunk, i)][:], in1=bias_sum[:], op=mybir.AluOpType.add
                 )
-                nc.sync.dma_start(out=out_rows[:, chunk * TILES_PER_CHUNK + i, :], in_=result[:])
+                nc.sync.dma_start(out=out_rows[:, CHUNK_FIRST[chunk] + i, :], in_=result[:])
 
         for r in range(LOAD_AHEAD):
             load_round(r)
-        for step in rounds[0]:
-            sort_words(step)
+        sort_round(0)
         for r in range(n_rounds + 2):
             if r + LOAD_AHEAD < n_rounds:
                 load_round(r + LOAD_AHEAD)
-            if r >= 2:
-                chunk, slot = rounds[r - 2][-1]
-                if slot == SLOTS - 1:
-                    finish(chunk)
+            if r >= 2 and rounds[r - 2][2] == SLOTS:
+                finish(rounds[r - 2][0])
             if r < n_rounds:
-                for step in rounds[r]:
-                    turn(step)
+                turn_round(r)
             if 1 <= r <= n_rounds:
-                multiply(rounds[r - 1])
+                multiply_round(r - 1)
             if r == BIAS_TURN:
                 sum_biases()
-            to_sort = rounds[r + 1] if r + 1 < n_rounds else []
-            to_quantise = rounds[r] if r < n_rounds else []
-            for step in to_sort:
-                sort_words(step)
-            for step in to_quantise:
-                quantise(step)
+            if r + 1 < n_rounds:
+                sort_round(r + 1)
+            if r < n_rounds:
+                quantise_round(r)

@@ -26,12 +26,12 @@ CHUNK_FIRST = [sum(CHUNK_TILES[:c]) for c in range(len(CHUNK_TILES))]
 UNITS_PER_BANK = 2
 UNITS_PER_COPY = 4
 
-WIDE_CUTS = [0, 1, 3, 5, 7, 9]
-NARROW_CUTS = [0, 4, 9]
-MAX_UNITS = 10
+RUN_UNITS = 6
+HEAD_RUNS = [4, 8]
+MAX_UNITS = 8
 WIDE_BANKS = [4, 5, 6, 7]
 NARROW_BANKS = [4, 5, 6, 7, 0, 1]
-LOAD_AHEAD = 6
+LOAD_AHEAD = 8
 BIAS_TURN = 2
 
 FLOPS = 2 * ROWS * SLOTS * C_IN * C_OUT
@@ -48,7 +48,9 @@ def tile_scattervertical_e_kernel(
 
     rounds = []
     for chunk, n_tiles in enumerate(CHUNK_TILES):
-        cuts = WIDE_CUTS if n_tiles == 4 else NARROW_CUTS
+        end = SLOTS * n_tiles
+        cuts = [0, HEAD_RUNS[0]] if chunk == 0 else [0]
+        cuts.extend(range(sum(HEAD_RUNS) if chunk == 0 else RUN_UNITS, end + 1, RUN_UNITS))
         rounds.extend([(chunk, a, b) for a, b in zip(cuts, cuts[1:])])
     n_rounds = len(rounds)
 
@@ -59,7 +61,7 @@ def tile_scattervertical_e_kernel(
         sorted_pool = ctx.enter_context(tc.tile_pool(name="sorted", bufs=2))
         grouped_pool = ctx.enter_context(tc.tile_pool(name="grouped", bufs=2))
         codes_pool = ctx.enter_context(tc.tile_pool(name="codes", bufs=2))
-        result_pool = ctx.enter_context(tc.tile_pool(name="result", bufs=4))
+        result_pool = ctx.enter_context(tc.tile_pool(name="result", bufs=8))
         psum = ctx.enter_context(tc.psum_pool(name="psum", bufs=1))
 
         identity = keep.tile([P, P], F32)
@@ -131,37 +133,43 @@ def tile_scattervertical_e_kernel(
                 in_=weights_words[slot].rearrange("p n t -> p (n t)").bitcast(I32),
             )
 
-        def load_round(r):
+        def slots_touched(r):
             chunk, a, b = rounds[r]
-            for slot in range(a, b):
+            n_tiles = CHUNK_TILES[chunk]
+            return range(-(-a // n_tiles), -(-b // n_tiles))
+
+        def load_round(r):
+            chunk = rounds[r][0]
+            for slot in slots_touched(r):
                 load_x(chunk, slot)
             if r == 1:
                 load_scale_rows()
             if r == 2:
                 nc.sync.dma_start(out=bias_rows[0:SLOTS, :], in_=bias)
             if r >= 1:
-                chunk, a, b = rounds[r - 1]
-                if chunk == 0:
-                    for slot in range(a, b):
+                if rounds[r - 1][0] == 0:
+                    for slot in slots_touched(r - 1):
                         load_codes(slot)
 
         def sort_round(r):
             chunk, a, b = rounds[r]
-            n_tiles = CHUNK_TILES[chunk]
             sorted_words = sorted_pool.tile([P, MAX_UNITS, HALVES, P], F32)
-            slots = UNITS_PER_COPY // n_tiles
-            for s in range(a, b, slots):
-                e = min(s + slots, b)
-                words = raw_tiles[chunk][:, s:e, :, :].rearrange("p s i c -> p (s i c)").bitcast(F32)
+            words = (
+                raw_tiles[chunk][:]
+                .rearrange("p s i c -> p (s i c)")
+                .bitcast(F32)
+                .rearrange("p (k j u) -> p k u j", j=P, u=HALVES)
+            )
+            for first in range(a, b, UNITS_PER_COPY):
+                end = min(first + UNITS_PER_COPY, b)
                 nc.vector.tensor_copy(
-                    out=sorted_words[:, (s - a) * n_tiles : (e - a) * n_tiles, :, :],
-                    in_=words.rearrange("p (k j u) -> p k u j", j=P, u=HALVES),
+                    out=sorted_words[:, first - a : end - a, :, :], in_=words[:, first:end, :, :]
                 )
             sorted_tiles[r] = sorted_words
 
         def n_units(r):
             chunk, a, b = rounds[r]
-            return (b - a) * CHUNK_TILES[chunk]
+            return b - a
 
         def turn_round(r):
             grouped = grouped_pool.tile([P, MAX_UNITS, P, PACK], BF16, align_bytes=64)
@@ -202,10 +210,12 @@ def tile_scattervertical_e_kernel(
             n_tiles = CHUNK_TILES[chunk]
             x_codes, x_scales = code_tiles[r]
             for i in range(n_tiles):
-                for slot in range(a, b):
+                for k in range(b - a):
+                    slot, tile = divmod(a + k, n_tiles)
+                    if tile != i:
+                        continue
                     if slot == 0:
                         sums[(chunk, i)] = sum_bank(chunk, i)
-                    k = (slot - a) * n_tiles + i
                     nc.tensor.matmul_mx(
                         out=sums[(chunk, i)][:],
                         lhsT=x_codes[:, k, :].bitcast(FP8X4),
@@ -230,7 +240,7 @@ def tile_scattervertical_e_kernel(
         for r in range(n_rounds + 2):
             if r + LOAD_AHEAD < n_rounds:
                 load_round(r + LOAD_AHEAD)
-            if r >= 2 and rounds[r - 2][2] == SLOTS:
+            if r >= 2 and rounds[r - 2][2] == SLOTS * CHUNK_TILES[rounds[r - 2][0]]:
                 finish(rounds[r - 2][0])
             if r < n_rounds:
                 turn_round(r)

@@ -21,18 +21,20 @@ ROW_TILES = ROWS // P
 SCALE_ROWS = 16
 QUADRANTS = 4
 
-CHUNK_TILES = [4, 2, 2, 2, 2, 2, 2]
+CHUNK_TILES = [4, 3, 3, 3, 3]
 CHUNK_FIRST = [sum(CHUNK_TILES[:c]) for c in range(len(CHUNK_TILES))]
 UNITS_PER_BANK = 2
 UNITS_PER_COPY = 4
 
-RUN_UNITS = 6
-HEAD_RUNS = [4, 8]
-MAX_UNITS = 8
-WIDE_BANKS = [4, 5, 6, 7]
-NARROW_BANKS = [4, 5, 6, 7, 0, 1]
-LOAD_AHEAD = 8
-BIAS_TURN = 2
+WIDE_RUNS = [4, 4, 4, 6, 6, 6, 6]
+NARROW_RUNS = [7, 7, 7, 6]
+MAX_UNITS = 7
+TURN_BANKS = [4, 5, 6, 7]
+SUM_BANKS = [0, 1, 2, 3]
+LOAD_AHEAD = 9
+LAST_PARTS = 2
+PART_BANK = 0
+BIAS_TURN = 5
 
 FLOPS = 2 * ROWS * SLOTS * C_IN * C_OUT
 
@@ -48,16 +50,15 @@ def tile_scattervertical_e_kernel(
 
     rounds = []
     for chunk, n_tiles in enumerate(CHUNK_TILES):
-        end = SLOTS * n_tiles
-        cuts = [0, HEAD_RUNS[0]] if chunk == 0 else [0]
-        cuts.extend(range(sum(HEAD_RUNS) if chunk == 0 else RUN_UNITS, end + 1, RUN_UNITS))
+        runs = WIDE_RUNS if chunk == 0 else NARROW_RUNS
+        cuts = [sum(runs[:h]) for h in range(len(runs) + 1)]
         rounds.extend([(chunk, a, b) for a, b in zip(cuts, cuts[1:])])
     n_rounds = len(rounds)
 
     with ExitStack() as ctx:
         ctx.enter_context(tc.manual_schedule())
         keep = ctx.enter_context(tc.tile_pool(name="keep", bufs=1))
-        raw_pool = ctx.enter_context(tc.tile_pool(name="raw", bufs=4))
+        raw_pool = ctx.enter_context(tc.tile_pool(name="raw", bufs=3))
         sorted_pool = ctx.enter_context(tc.tile_pool(name="sorted", bufs=2))
         grouped_pool = ctx.enter_context(tc.tile_pool(name="grouped", bufs=2))
         codes_pool = ctx.enter_context(tc.tile_pool(name="codes", bufs=2))
@@ -79,22 +80,29 @@ def tile_scattervertical_e_kernel(
         first_copy = keep.tile([P, 1], BF16)
         nc.scalar.copy(out=first_copy[:], in_=ones[:, 0:1])
 
-        turns_made = {"wide": 0, "narrow": 0}
+        turns_made = [0]
 
         def open_bank(number):
             return psum.tile([P, C_OUT], F32, name="bank%d" % number)
 
-        def next_turn_bank(chunk):
-            kind, banks = ("wide", WIDE_BANKS) if chunk == 0 else ("narrow", NARROW_BANKS)
-            number = banks[turns_made[kind] % len(banks)]
-            turns_made[kind] += 1
+        def next_turn_bank():
+            number = TURN_BANKS[turns_made[0] % len(TURN_BANKS)]
+            turns_made[0] += 1
             return open_bank(number)
 
-        def sum_bank(chunk, i):
-            return open_bank(i if chunk == 0 else 2 + i)
+        def n_parts(chunk, i):
+            return LAST_PARTS if (chunk, i) == (len(CHUNK_TILES) - 1, CHUNK_TILES[-1] - 1) else 1
+
+        def sum_bank(chunk, i, part):
+            if part > 0:
+                return open_bank(PART_BANK)
+            if chunk == 0:
+                return open_bank(i)
+            done = CHUNK_FIRST[chunk] - CHUNK_TILES[0]
+            return open_bank(SUM_BANKS[(done + i) % len(SUM_BANKS)])
 
         def sum_biases():
-            bias_bank = next_turn_bank(0)
+            bias_bank = next_turn_bank()
             nc.tensor.matmul(
                 out=bias_bank[:], lhsT=ones[:], rhs=bias_rows[:], start=True, stop=True
             )
@@ -113,10 +121,13 @@ def tile_scattervertical_e_kernel(
                     raw_tiles[chunk] = keep.tile([P, SLOTS, n_tiles, C_IN], BF16, name="wide_raw")
                 else:
                     raw_tiles[chunk] = raw_pool.tile([P, SLOTS, n_tiles, C_IN], BF16, name="raw")
-            nc.sync.dma_start(
-                out=raw_tiles[chunk][:, slot, :, :],
-                in_=x_rows[slot][:, first : first + n_tiles, :],
-            )
+            parts = 2 if (chunk, slot) == (0, 0) else 1
+            width = n_tiles // parts
+            for i in range(0, n_tiles, width):
+                nc.sync.dma_start(
+                    out=raw_tiles[chunk][:, slot, i : i + width, :],
+                    in_=x_rows[slot][:, first + i : first + i + width, :],
+                )
 
         def load_scale_rows():
             for quadrant in range(QUADRANTS):
@@ -142,13 +153,14 @@ def tile_scattervertical_e_kernel(
             chunk = rounds[r][0]
             for slot in slots_touched(r):
                 load_x(chunk, slot)
-            if r == 1:
-                load_scale_rows()
-            if r == 2:
-                nc.sync.dma_start(out=bias_rows[0:SLOTS, :], in_=bias)
-            if r >= 1:
-                if rounds[r - 1][0] == 0:
-                    for slot in slots_touched(r - 1):
+                if chunk == 0:
+                    if slot == 1:
+                        load_scale_rows()
+                    if slot == 4:
+                        nc.sync.dma_start(out=bias_rows[0:SLOTS, :], in_=bias)
+                    if slot >= 1:
+                        load_codes(slot - 1)
+                    if slot == SLOTS - 1:
                         load_codes(slot)
 
         def sort_round(r):
@@ -160,11 +172,14 @@ def tile_scattervertical_e_kernel(
                 .bitcast(F32)
                 .rearrange("p (k j u) -> p k u j", j=P, u=HALVES)
             )
-            for first in range(a, b, UNITS_PER_COPY):
-                end = min(first + UNITS_PER_COPY, b)
+            first = a
+            while first < b:
+                count = max(c for c in (2 if r == 0 else 4, 2, 1) if c <= b - first)
                 nc.vector.tensor_copy(
-                    out=sorted_words[:, first - a : end - a, :, :], in_=words[:, first:end, :, :]
+                    out=sorted_words[:, first - a : first - a + count, :, :],
+                    in_=words[:, first : first + count, :, :],
                 )
+                first += count
             sorted_tiles[r] = sorted_words
 
         def n_units(r):
@@ -180,24 +195,28 @@ def tile_scattervertical_e_kernel(
                 .rearrange("p (k r u) -> p k r u", k=MAX_UNITS, u=HALVES)
             )
             for first in range(0, n_units(r), UNITS_PER_BANK):
-                bank = next_turn_bank(rounds[r][0])
+                bank = next_turn_bank()
                 turned = bank[:].rearrange("p (k u r) -> p k u r", k=UNITS_PER_BANK, u=HALVES)
-                for k in range(UNITS_PER_BANK):
+                count = min(UNITS_PER_BANK, n_units(r) - first)
+                for k in range(count):
                     for u in range(HALVES):
                         nc.tensor.transpose(
                             turned[:, k, u, :], sorted_tiles[r][:, first + k, u, :], identity[:]
                         )
                 nc.scalar.copy(
-                    out=grouped_words[:, first : first + UNITS_PER_BANK, :, :],
-                    in_=turned.rearrange("p k u r -> p k r u"),
+                    out=grouped_words[:, first : first + count, :, :],
+                    in_=turned[:, 0:count, :, :].rearrange("p k u r -> p k r u"),
                 )
             grouped_tiles[r] = grouped
 
         def quantise_round(r):
             x_codes = codes_pool.tile([P, MAX_UNITS, P], U32, align_bytes=64)
             x_scales = codes_pool.tile([P, MAX_UNITS, P], U8, align_bytes=64)
-            for first in range(0, n_units(r), UNITS_PER_COPY):
-                units = slice(first, min(first + UNITS_PER_COPY, n_units(r)))
+            first = 0
+            while first < n_units(r):
+                count = max(c for c in (4, 2, 1) if c <= n_units(r) - first)
+                units = slice(first, first + count)
+                first += count
                 nc.vector.quantize_mx(
                     out=x_codes[:, units, :].rearrange("p k r -> p (k r)").bitcast(FP8X4),
                     scales=x_scales[:, units, :].rearrange("p k r -> p (k r)"),
@@ -210,29 +229,42 @@ def tile_scattervertical_e_kernel(
             n_tiles = CHUNK_TILES[chunk]
             x_codes, x_scales = code_tiles[r]
             for i in range(n_tiles):
-                for k in range(b - a):
-                    slot, tile = divmod(a + k, n_tiles)
-                    if tile != i:
-                        continue
-                    if slot == 0:
-                        sums[(chunk, i)] = sum_bank(chunk, i)
-                    nc.tensor.matmul_mx(
-                        out=sums[(chunk, i)][:],
-                        lhsT=x_codes[:, k, :].bitcast(FP8X4),
-                        lhsT_scale=x_scales[:, k, :],
-                        rhs=w_codes[:, slot, :].bitcast(FP8X4),
-                        rhs_scale=w_scales[:, slot, :],
-                        start=(slot == 0),
-                        stop=(slot == SLOTS - 1),
-                    )
+                parts = n_parts(chunk, i)
+                width = C_OUT // parts
+                for part in range(parts):
+                    cols = slice(part * width, (part + 1) * width)
+                    for k in range(b - a):
+                        slot, tile = divmod(a + k, n_tiles)
+                        if tile != i:
+                            continue
+                        if slot == 0:
+                            sums[(chunk, i, part)] = sum_bank(chunk, i, part)
+                        nc.tensor.matmul_mx(
+                            out=sums[(chunk, i, part)][:, 0:width],
+                            lhsT=x_codes[:, k, :].bitcast(FP8X4),
+                            lhsT_scale=x_scales[:, k, :],
+                            rhs=w_codes[:, slot, PACK * cols.start : PACK * cols.stop].bitcast(FP8X4),
+                            rhs_scale=w_scales[:, slot, cols],
+                            start=(slot == 0),
+                            stop=(slot == SLOTS - 1),
+                        )
 
         def finish(chunk):
             for i in range(CHUNK_TILES[chunk]):
-                result = result_pool.tile([P, C_OUT], F32)
-                nc.vector.tensor_tensor(
-                    out=result[:], in0=sums[(chunk, i)][:], in1=bias_sum[:], op=mybir.AluOpType.add
-                )
-                nc.sync.dma_start(out=out_rows[:, CHUNK_FIRST[chunk] + i, :], in_=result[:])
+                parts = n_parts(chunk, i)
+                width = C_OUT // parts
+                for part in range(parts):
+                    cols = slice(part * width, (part + 1) * width)
+                    result = result_pool.tile([P, C_OUT], F32)
+                    nc.vector.tensor_tensor(
+                        out=result[:, 0:width],
+                        in0=sums[(chunk, i, part)][:, 0:width],
+                        in1=bias_sum[:, cols],
+                        op=mybir.AluOpType.add,
+                    )
+                    nc.sync.dma_start(
+                        out=out_rows[:, CHUNK_FIRST[chunk] + i, cols], in_=result[:, 0:width]
+                    )
 
         for r in range(LOAD_AHEAD):
             load_round(r)

@@ -68,8 +68,8 @@ def tile_scattervertical_e_kernel(
         identity = keep.tile([P, P], F32)
         make_identity(nc, identity[:])
 
-        w_codes = keep.tile([P, SLOTS, C_OUT * PACK], U8, align_bytes=64)
-        w_scales = keep.tile([P, SLOTS, C_OUT], U8, align_bytes=64)
+        w_codes = keep.tile([P, SLOTS, C_OUT * PACK], U8, align_bytes=256)
+        w_scales = keep.tile([P, SLOTS, C_OUT], U8, align_bytes=256)
         nc.vector.memset(w_scales[:].bitcast(I32), 0)
 
         bias_rows = keep.tile([P, C_OUT], BF16)
@@ -210,8 +210,8 @@ def tile_scattervertical_e_kernel(
             grouped_tiles[r] = grouped
 
         def quantise_round(r):
-            x_codes = codes_pool.tile([P, MAX_UNITS, P], U32, align_bytes=64)
-            x_scales = codes_pool.tile([P, MAX_UNITS, P], U8, align_bytes=64)
+            x_codes = codes_pool.tile([P, MAX_UNITS, P], U32, align_bytes=256)
+            x_scales = codes_pool.tile([P, MAX_UNITS, P], U8, align_bytes=256)
             first = 0
             while first < n_units(r):
                 count = max(c for c in (4, 2, 1) if c <= n_units(r) - first)

@@ -19,6 +19,8 @@ C_IN = 512
 C_OUT = 512
 ROW_TILES = ROWS // P
 SCALE_ROWS = 16
+SLOTS_PER_PLANE = 4
+SCALE_GROUPS = -(-SLOTS // SLOTS_PER_PLANE)
 QUADRANTS = 4
 
 CHUNK_TILES = [4, 3, 3, 3, 3]
@@ -65,11 +67,11 @@ def tile_scattervertical_e_kernel(
         result_pool = ctx.enter_context(tc.tile_pool(name="result", bufs=8))
         psum = ctx.enter_context(tc.psum_pool(name="psum", bufs=1))
 
-        identity = keep.tile([P, P], F32)
+        identity = keep.tile([P, P], F32, align_bytes=256)
         make_identity(nc, identity[:])
 
         w_codes = keep.tile([P, SLOTS, C_OUT * PACK], U8, align_bytes=256)
-        w_scales = keep.tile([P, SLOTS, C_OUT], U8, align_bytes=256)
+        w_scales = keep.tile([P, SCALE_GROUPS, C_OUT], U8, align_bytes=256)
         nc.vector.memset(w_scales[:].bitcast(I32), 0)
 
         bias_rows = keep.tile([P, C_OUT], BF16)
@@ -129,13 +131,14 @@ def tile_scattervertical_e_kernel(
                     in_=x_rows[slot][:, first + i : first + i + width, :],
                 )
 
-        def load_scale_rows():
+        def load_scale_rows(group):
+            first = group * SLOTS_PER_PLANE
+            end = min(first + SLOTS_PER_PLANE, SLOTS)
             for quadrant in range(QUADRANTS):
+                rows = slice(32 * quadrant, 32 * quadrant + 4 * (end - first))
                 nc.sync.dma_start(
-                    out=w_scales[32 * quadrant : 32 * quadrant + 4, :, :].bitcast(I32),
-                    in_=weights_scales[:, 4 * quadrant : 4 * quadrant + 4, :]
-                    .rearrange("g r n -> r g n")
-                    .bitcast(I32),
+                    out=w_scales[rows, group, :].bitcast(I32),
+                    in_=weights_scales[first:end, 4 * quadrant : 4 * quadrant + 4, :].bitcast(I32),
                 )
 
         def load_codes(slot):
@@ -155,7 +158,11 @@ def tile_scattervertical_e_kernel(
                 load_x(chunk, slot)
                 if chunk == 0:
                     if slot == 1:
-                        load_scale_rows()
+                        load_scale_rows(0)
+                    if slot == 3:
+                        load_scale_rows(1)
+                    if slot == 6:
+                        load_scale_rows(2)
                     if slot == 4:
                         nc.sync.dma_start(out=bias_rows[0:SLOTS, :], in_=bias)
                     if slot >= 1:
@@ -165,7 +172,7 @@ def tile_scattervertical_e_kernel(
 
         def sort_round(r):
             chunk, a, b = rounds[r]
-            sorted_words = sorted_pool.tile([P, MAX_UNITS, HALVES, P], F32)
+            sorted_words = sorted_pool.tile([P, MAX_UNITS, HALVES, P], F32, align_bytes=256)
             words = (
                 raw_tiles[chunk][:]
                 .rearrange("p s i c -> p (s i c)")
@@ -244,7 +251,9 @@ def tile_scattervertical_e_kernel(
                             lhsT=x_codes[:, k, :].bitcast(FP8X4),
                             lhsT_scale=x_scales[:, k, :],
                             rhs=w_codes[:, slot, PACK * cols.start : PACK * cols.stop].bitcast(FP8X4),
-                            rhs_scale=w_scales[:, slot, cols],
+                            rhs_scale=w_scales[
+                                4 * (slot % SLOTS_PER_PLANE) : P, slot // SLOTS_PER_PLANE, cols
+                            ],
                             start=(slot == 0),
                             stop=(slot == SLOTS - 1),
                         )

@@ -35,6 +35,7 @@ TURN_BANKS = [4, 5, 6, 7]
 SUM_BANKS = [0, 1, 2, 3]
 LOAD_AHEAD = 9
 LAST_PARTS = 2
+WARM_UP = 4
 PART_BANK = 0
 BIAS_TURN = 5
 
@@ -67,6 +68,10 @@ def tile_scattervertical_e_kernel(
         result_pool = ctx.enter_context(tc.tile_pool(name="result", bufs=8))
         psum = ctx.enter_context(tc.psum_pool(name="psum", bufs=1))
 
+        ones = keep.tile([P, P], BF16, align_bytes=256)
+        zeros = keep.tile([P, C_OUT], BF16, align_bytes=256)
+        nc.gpsimd.memset(ones[:], 1.0)
+        nc.vector.memset(zeros[:].bitcast(I32), 0)
         identity = keep.tile([P, P], F32, align_bytes=256)
         make_identity(nc, identity[:])
 
@@ -74,11 +79,9 @@ def tile_scattervertical_e_kernel(
         w_scales = keep.tile([P, SCALE_GROUPS, C_OUT], U8, align_bytes=256)
         nc.vector.memset(w_scales[:].bitcast(I32), 0)
 
-        bias_rows = keep.tile([P, C_OUT], BF16)
-        ones = keep.tile([P, P], BF16)
-        bias_sum = keep.tile([P, C_OUT], F32)
+        bias_rows = keep.tile([P, C_OUT], BF16, align_bytes=256)
+        bias_sum = keep.tile([P, C_OUT], F32, align_bytes=256)
         nc.vector.memset(bias_rows[:].bitcast(I32), 0)
-        nc.gpsimd.memset(ones[:], 1.0)
         first_copy = keep.tile([P, 1], BF16)
         nc.scalar.copy(out=first_copy[:], in_=ones[:, 0:1])
 
@@ -103,6 +106,13 @@ def tile_scattervertical_e_kernel(
             done = CHUNK_FIRST[chunk] - CHUNK_TILES[0]
             return open_bank(SUM_BANKS[(done + i) % len(SUM_BANKS)])
 
+        def warm_up():
+            bank = open_bank(TURN_BANKS[-1])
+            for k in range(WARM_UP):
+                nc.tensor.matmul(
+                    out=bank[:], lhsT=ones[:], rhs=zeros[:], start=True, stop=True
+                )
+
         def sum_biases():
             bias_bank = next_turn_bank()
             nc.tensor.matmul(
@@ -120,9 +130,11 @@ def tile_scattervertical_e_kernel(
             first, n_tiles = CHUNK_FIRST[chunk], CHUNK_TILES[chunk]
             if slot == 0:
                 if chunk == 0:
-                    raw_tiles[chunk] = keep.tile([P, SLOTS, n_tiles, C_IN], BF16, name="wide_raw")
+                    raw_tiles[chunk] = keep.tile([P, SLOTS, n_tiles, C_IN], BF16, name="wide_raw", align_bytes=256)
                 else:
-                    raw_tiles[chunk] = raw_pool.tile([P, SLOTS, n_tiles, C_IN], BF16, name="raw")
+                    raw_tiles[chunk] = raw_pool.tile(
+                        [P, SLOTS, n_tiles, C_IN], BF16, name="raw", align_bytes=256
+                    )
             parts = 2 if (chunk, slot) == (0, 0) else 1
             width = n_tiles // parts
             for i in range(0, n_tiles, width):
@@ -181,7 +193,7 @@ def tile_scattervertical_e_kernel(
             )
             first = a
             while first < b:
-                count = max(c for c in (2 if r == 0 else 4, 2, 1) if c <= b - first)
+                count = max(c for c in (2 if chunk == 0 else 4, 2, 1) if c <= b - first)
                 nc.vector.tensor_copy(
                     out=sorted_words[:, first - a : first - a + count, :, :],
                     in_=words[:, first : first + count, :, :],
@@ -194,7 +206,7 @@ def tile_scattervertical_e_kernel(
             return b - a
 
         def turn_round(r):
-            grouped = grouped_pool.tile([P, MAX_UNITS, P, PACK], BF16, align_bytes=64)
+            grouped = grouped_pool.tile([P, MAX_UNITS, P, PACK], BF16, align_bytes=256)
             grouped_words = (
                 grouped[:]
                 .rearrange("p k r t -> p (k r t)")
@@ -221,7 +233,7 @@ def tile_scattervertical_e_kernel(
             x_scales = codes_pool.tile([P, MAX_UNITS, P], U8, align_bytes=256)
             first = 0
             while first < n_units(r):
-                count = max(c for c in (4, 2, 1) if c <= n_units(r) - first)
+                count = max(c for c in (2 if rounds[r][0] == 0 else 4, 2, 1) if c <= n_units(r) - first)
                 units = slice(first, first + count)
                 first += count
                 nc.vector.quantize_mx(
@@ -264,7 +276,7 @@ def tile_scattervertical_e_kernel(
                 width = C_OUT // parts
                 for part in range(parts):
                     cols = slice(part * width, (part + 1) * width)
-                    result = result_pool.tile([P, C_OUT], F32)
+                    result = result_pool.tile([P, C_OUT], F32, align_bytes=256)
                     nc.vector.tensor_tensor(
                         out=result[:, 0:width],
                         in0=sums[(chunk, i, part)][:, 0:width],
@@ -278,6 +290,7 @@ def tile_scattervertical_e_kernel(
         for r in range(LOAD_AHEAD):
             load_round(r)
         sort_round(0)
+        warm_up()
         for r in range(n_rounds + 2):
             if r + LOAD_AHEAD < n_rounds:
                 load_round(r + LOAD_AHEAD)

from contextlib import ExitStack

import concourse.mybir as mybir
from concourse.masks import make_identity

F32 = mybir.dt.float32
BF16 = mybir.dt.bfloat16
I32 = mybir.dt.int32
U32 = mybir.dt.uint32
U8 = mybir.dt.uint8
FP8X4 = mybir.dt.float8_e4m3fn_x4

P = 128
PACK = 4
HALVES = 2
SLOTS = 9
ROWS = 2048
C_IN = 512
C_OUT = 512
ROW_TILES = ROWS // P
SCALE_ROWS = 16
SLOTS_PER_PLANE = 4
SCALE_GROUPS = -(-SLOTS // SLOTS_PER_PLANE)
QUADRANTS = 4

CHUNK_TILES = [4, 3, 3, 3, 3]
CHUNK_FIRST = [sum(CHUNK_TILES[:c]) for c in range(len(CHUNK_TILES))]
UNITS_PER_BANK = 2
UNITS_PER_COPY = 4

WIDE_RUNS = [4, 4, 4, 6, 6, 6, 6]
NARROW_RUNS = [7, 7, 7, 6]
MAX_UNITS = 7
TURN_BANKS = [4, 5, 6, 7]
SUM_BANKS = [0, 1, 2, 3]
LOAD_AHEAD = 9
LAST_PARTS = 2
WARM_UP = 4
PART_BANK = 0
BIAS_TURN = 5

FLOPS = 2 * ROWS * SLOTS * C_IN * C_OUT


def tile_scattervertical_e_kernel(
    tc, x0, x1, x2, x3, x4, x5, x6, x7, x8, weights_words, weights_scales, bias, out
):
    nc = tc.nc
    x_rows = [
        x.rearrange("(p t) c -> p t c", t=ROW_TILES) for x in (x0, x1, x2, x3, x4, x5, x6, x7, x8)
    ]
    out_rows = out.rearrange("(p t) o -> p t o", t=ROW_TILES)

    rounds = []
    for chunk, n_tiles in enumerate(CHUNK_TILES):
        runs = WIDE_RUNS if chunk == 0 else NARROW_RUNS
        cuts = [sum(runs[:h]) for h in range(len(runs) + 1)]
        rounds.extend([(chunk, a, b) for a, b in zip(cuts, cuts[1:])])
    n_rounds = len(rounds)

    with ExitStack() as ctx:
        ctx.enter_context(tc.manual_schedule())
        keep = ctx.enter_context(tc.tile_pool(name="keep", bufs=1))
        raw_pool = ctx.enter_context(tc.tile_pool(name="raw", bufs=3))
        sorted_pool = ctx.enter_context(tc.tile_pool(name="sorted", bufs=2))
        grouped_pool = ctx.enter_context(tc.tile_pool(name="grouped", bufs=2))
        codes_pool = ctx.enter_context(tc.tile_pool(name="codes", bufs=2))
        result_pool = ctx.enter_context(tc.tile_pool(name="result", bufs=8))
        psum = ctx.enter_context(tc.psum_pool(name="psum", bufs=1))

        ones = keep.tile([P, P], BF16, align_bytes=256)
        zeros = keep.tile([P, C_OUT], BF16, align_bytes=256)
        nc.gpsimd.memset(ones[:], 1.0)
        nc.vector.memset(zeros[:].bitcast(I32), 0)
        identity = keep.tile([P, P], F32, align_bytes=256)
        make_identity(nc, identity[:])

        w_codes = keep.tile([P, SLOTS, C_OUT * PACK], U8, align_bytes=256)
        w_scales = keep.tile([P, SCALE_GROUPS, C_OUT], U8, align_bytes=256)
        nc.vector.memset(w_scales[:].bitcast(I32), 0)

        bias_rows = keep.tile([P, C_OUT], BF16, align_bytes=256)
        bias_sum = keep.tile([P, C_OUT], F32, align_bytes=256)
        nc.vector.memset(bias_rows[:].bitcast(I32), 0)
        first_copy = keep.tile([P, 1], BF16)
        nc.scalar.copy(out=first_copy[:], in_=ones[:, 0:1])

        turns_made = [0]

        def open_bank(number):
            return psum.tile([P, C_OUT], F32, name="bank%d" % number)

        def next_turn_bank():
            number = TURN_BANKS[turns_made[0] % len(TURN_BANKS)]
            turns_made[0] += 1
            return open_bank(number)

        def n_parts(chunk, i):
            return LAST_PARTS if (chunk, i) == (len(CHUNK_TILES) - 1, CHUNK_TILES[-1] - 1) else 1

        def sum_bank(chunk, i, part):
            if part > 0:
                return open_bank(PART_BANK)
            if chunk == 0:
                return open_bank(i)
            done = CHUNK_FIRST[chunk] - CHUNK_TILES[0]
            return open_bank(SUM_BANKS[(done + i) % len(SUM_BANKS)])

        def warm_up():
            bank = open_bank(TURN_BANKS[-1])
            for k in range(WARM_UP):
                nc.tensor.matmul(
                    out=bank[:], lhsT=ones[:], rhs=zeros[:], start=True, stop=True
                )

        def sum_biases():
            bias_bank = next_turn_bank()
            nc.tensor.matmul(
                out=bias_bank[:], lhsT=ones[:], rhs=bias_rows[:], start=True, stop=True
            )
            nc.scalar.copy(out=bias_sum[:], in_=bias_bank[:])

        raw_tiles = {}
        sorted_tiles = {}
        grouped_tiles = {}
        code_tiles = {}
        sums = {}

        def load_x(chunk, slot):
            first, n_tiles = CHUNK_FIRST[chunk], CHUNK_TILES[chunk]
            if slot == 0:
                if chunk == 0:
                    raw_tiles[chunk] = keep.tile([P, SLOTS, n_tiles, C_IN], BF16, name="wide_raw", align_bytes=256)
                else:
                    raw_tiles[chunk] = raw_pool.tile(
                        [P, SLOTS, n_tiles, C_IN], BF16, name="raw", align_bytes=256
                    )
            parts = 2 if (chunk, slot) == (0, 0) else 1
            width = n_tiles // parts
            for i in range(0, n_tiles, width):
                nc.sync.dma_start(
                    out=raw_tiles[chunk][:, slot, i : i + width, :],
                    in_=x_rows[slot][:, first + i : first + i + width, :],
                )

        def load_scale_rows(group):
            first = group * SLOTS_PER_PLANE
            end = min(first + SLOTS_PER_PLANE, SLOTS)
            for quadrant in range(QUADRANTS):
                rows = slice(32 * quadrant, 32 * quadrant + 4 * (end - first))
                nc.sync.dma_start(
                    out=w_scales[rows, group, :].bitcast(I32),
                    in_=weights_scales[first:end, 4 * quadrant : 4 * quadrant + 4, :].bitcast(I32),
                )

        def load_codes(slot):
            nc.sync.dma_start(
                out=w_codes[:, slot, :].bitcast(I32),
                in_=weights_words[slot].rearrange("p n t -> p (n t)").bitcast(I32),
            )

        def slots_touched(r):
            chunk, a, b = rounds[r]
            n_tiles = CHUNK_TILES[chunk]
            return range(-(-a // n_tiles), -(-b // n_tiles))

        def load_round(r):
            chunk = rounds[r][0]
            for slot in slots_touched(r):
                load_x(chunk, slot)
                if chunk == 0:
                    if slot == 1:
                        load_scale_rows(0)
                    if slot == 3:
                        load_scale_rows(1)
                    if slot == 6:
                        load_scale_rows(2)
                    if slot == 4:
                        nc.sync.dma_start(out=bias_rows[0:SLOTS, :], in_=bias)
                    if slot >= 1:
                        load_codes(slot - 1)
                    if slot == SLOTS - 1:
                        load_codes(slot)

        def sort_round(r):
            chunk, a, b = rounds[r]
            sorted_words = sorted_pool.tile([P, MAX_UNITS, HALVES, P], F32, align_bytes=256)
            words = (
                raw_tiles[chunk][:]
                .rearrange("p s i c -> p (s i c)")
                .bitcast(F32)
                .rearrange("p (k j u) -> p k u j", j=P, u=HALVES)
            )
            first = a
            while first < b:
                count = max(c for c in (2 if chunk == 0 else 4, 2, 1) if c <= b - first)
                nc.vector.tensor_copy(
                    out=sorted_words[:, first - a : first - a + count, :, :],
                    in_=words[:, first : first + count, :, :],
                )
                first += count
            sorted_tiles[r] = sorted_words

        def n_units(r):
            chunk, a, b = rounds[r]
            return b - a

        def turn_round(r):
            grouped = grouped_pool.tile([P, MAX_UNITS, P, PACK], BF16, align_bytes=256)
            grouped_words = (
                grouped[:]
                .rearrange("p k r t -> p (k r t)")
                .bitcast(F32)
                .rearrange("p (k r u) -> p k r u", k=MAX_UNITS, u=HALVES)
            )
            for first in range(0, n_units(r), UNITS_PER_BANK):
                bank = next_turn_bank()
                turned = bank[:].rearrange("p (k u r) -> p k u r", k=UNITS_PER_BANK, u=HALVES)
                count = min(UNITS_PER_BANK, n_units(r) - first)
                for k in range(count):
                    for u in range(HALVES):
                        nc.tensor.transpose(
                            turned[:, k, u, :], sorted_tiles[r][:, first + k, u, :], identity[:]
                        )
                nc.scalar.copy(
                    out=grouped_words[:, first : first + count, :, :],
                    in_=turned[:, 0:count, :, :].rearrange("p k u r -> p k r u"),
                )
            grouped_tiles[r] = grouped

        def quantise_round(r):
            x_codes = codes_pool.tile([P, MAX_UNITS, P], U32, align_bytes=256)
            x_scales = codes_pool.tile([P, MAX_UNITS, P], U8, align_bytes=256)
            first = 0
            while first < n_units(r):
                count = max(c for c in (2 if rounds[r][0] == 0 else 4, 2, 1) if c <= n_units(r) - first)
                units = slice(first, first + count)
                first += count
                nc.vector.quantize_mx(
                    out=x_codes[:, units, :].rearrange("p k r -> p (k r)").bitcast(FP8X4),
                    scales=x_scales[:, units, :].rearrange("p k r -> p (k r)"),
                    in_=grouped_tiles[r][:, units, :, :].rearrange("p k r t -> p (k r t)"),
                )
            code_tiles[r] = (x_codes, x_scales)

        def multiply_round(r):
            chunk, a, b = rounds[r]
            n_tiles = CHUNK_TILES[chunk]
            x_codes, x_scales = code_tiles[r]
            for i in range(n_tiles):
                parts = n_parts(chunk, i)
                width = C_OUT // parts
                for part in range(parts):
                    cols = slice(part * width, (part + 1) * width)
                    for k in range(b - a):
                        slot, tile = divmod(a + k, n_tiles)
                        if tile != i:
                            continue
                        if slot == 0:
                            sums[(chunk, i, part)] = sum_bank(chunk, i, part)
                        nc.tensor.matmul_mx(
                            out=sums[(chunk, i, part)][:, 0:width],
                            lhsT=x_codes[:, k, :].bitcast(FP8X4),
                            lhsT_scale=x_scales[:, k, :],
                            rhs=w_codes[:, slot, PACK * cols.start : PACK * cols.stop].bitcast(FP8X4),
                            rhs_scale=w_scales[
                                4 * (slot % SLOTS_PER_PLANE) : P, slot // SLOTS_PER_PLANE, cols
                            ],
                            start=(slot == 0),
                            stop=(slot == SLOTS - 1),
                        )

        def finish(chunk):
            for i in range(CHUNK_TILES[chunk]):
                parts = n_parts(chunk, i)
                width = C_OUT // parts
                for part in range(parts):
                    cols = slice(part * width, (part + 1) * width)
                    result = result_pool.tile([P, C_OUT], F32, align_bytes=256)
                    nc.vector.tensor_tensor(
                        out=result[:, 0:width],
                        in0=sums[(chunk, i, part)][:, 0:width],
                        in1=bias_sum[:, cols],
                        op=mybir.AluOpType.add,
                    )
                    nc.sync.dma_start(
                        out=out_rows[:, CHUNK_FIRST[chunk] + i, cols], in_=result[:, 0:width]
                    )

        for r in range(LOAD_AHEAD):
            load_round(r)
        sort_round(0)
        warm_up()
        for r in range(n_rounds + 2):
            if r + LOAD_AHEAD < n_rounds:
                load_round(r + LOAD_AHEAD)
            if r >= 2 and rounds[r - 2][2] == SLOTS * CHUNK_TILES[rounds[r - 2][0]]:
                finish(rounds[r - 2][0])
            if r < n_rounds:
                turn_round(r)
            if 1 <= r <= n_rounds:
                multiply_round(r - 1)
            if r == BIAS_TURN:
                sum_biases()
            if r + 1 < n_rounds:
                sort_round(r + 1)
            if r < n_rounds:
                quantise_round(r)
